import numpy as np
import ml_dtypes

BF16 = ml_dtypes.bfloat16


def bf(x):
    return np.asarray(x, np.float32).astype(BF16)


def f32(x):
    return np.asarray(x, np.float32)


def f64(x):
    return np.asarray(x).astype(np.float64)


def striped(idx):
    return np.tile(idx.reshape(-1, 16).T, (8, 1))


C, E, K, M, S, N = 256, 256, 768, 768, 4096, 1024


def sigmoid(t):
    return 1.0 / (1.0 + np.exp(-t))


def setup_inputs():
    return {"base": f32(np.random.standard_normal((C, S))), "emb": bf(np.random.standard_normal((E, N))), "ctx": bf(np.random.standard_normal((K - E, N))), "h": bf(np.random.standard_normal((C, N))), "w_ih": bf(np.random.standard_normal((K, M)) / np.sqrt(K)), "w_hh": bf(np.random.standard_normal((C, M)) / np.sqrt(C)), "b_ih": f32(0.5 * np.random.standard_normal((M, 1))), "b_hh": f32(0.5 * np.random.standard_normal((M, 1))), "offs": striped(np.random.permutation(S)[:N])}


def reference(base, emb, ctx, h, w_ih, w_hh, b_ih, b_hh, offs):
    idx = offs[:16].T.reshape(-1)
    xin = np.concatenate([f64(emb), f64(ctx)], axis=0)
    u = f64(w_ih).T @ xin + f64(b_ih)
    v = f64(w_hh).T @ f64(h) + f64(b_hh)
    r = sigmoid(u[:C] + v[:C])
    z = sigmoid(u[C:M - C] + v[C:M - C])
    n = np.tanh(u[M - C:] + r * v[M - C:])
    fresh = (1.0 - z) * n
    kept = z * f64(h)
    out = f64(base).copy()
    out[:, idx] = fresh + kept
    return out

@@ -1,0 +1,118 @@
+import concourse.mybir as mybir
+
+F32 = mybir.dt.float32
+BF16 = mybir.dt.bfloat16
+U16 = mybir.dt.uint16
+ADD = mybir.AluOpType.add
+MULT = mybir.AluOpType.mult
+SIGMOID = mybir.ActivationFunctionType.Sigmoid
+TANH = mybir.ActivationFunctionType.Tanh
+
+P = 128
+CHANNELS = 256
+BLOCKS = CHANNELS // P
+EMB_ROWS = 256
+IN_ROWS = 768
+STREAMS = 1024
+SLOTS = 4096
+BANK = 512
+R, Z, N = 0, 1, 2
+
+FLOPS = 2 * STREAMS * 3 * CHANNELS * (IN_ROWS + CHANNELS)
+
+
+def accumulate(nc, bank, parts, gate_columns, streams):
+    for i, (weights, activations) in enumerate(parts):
+        nc.tensor.matmul(
+            bank[:],
+            weights[:, gate_columns],
+            activations[:, streams],
+            start=(i == 0),
+            stop=(i == len(parts) - 1),
+        )
+
+
+def tile_rnndecoder_kernel(tc, base, emb, ctx, h, w_ih, w_hh, b_ih, b_hh, offs, out):
+    nc = tc.nc
+    with (
+        tc.tile_pool(name="held", bufs=1) as held,
+        tc.tile_pool(name="work", bufs=2) as work,
+        tc.psum_pool(name="psum", bufs=2) as psum,
+    ):
+        offsets = held.tile([P, STREAMS // 16], U16, name="offsets")
+        nc.sync.dma_start(offsets[:], offs)
+
+        hidden_parts = []
+        for k in range(CHANNELS // P):
+            rows = slice(k * P, (k + 1) * P)
+            weights = held.tile([P, 3 * CHANNELS], BF16, name=f"w_hh{k}")
+            hidden = held.tile([P, STREAMS], BF16, name=f"h{k}")
+            nc.sync.dma_start(weights[:], w_hh[rows, :])
+            nc.scalar.dma_start(hidden[:], h[rows, :])
+            hidden_parts.append((weights, hidden))
+        input_parts = []
+        for k in range(IN_ROWS // P):
+            rows = slice(k * P, (k + 1) * P)
+            weights = held.tile([P, 3 * CHANNELS], BF16, name=f"w_ih{k}")
+            xin = held.tile([P, STREAMS], BF16, name=f"xin{k}")
+            nc.sync.dma_start(weights[:], w_ih[rows, :])
+            if k * P < EMB_ROWS:
+                nc.scalar.dma_start(xin[:], emb[rows, :])
+            else:
+                nc.scalar.dma_start(xin[:], ctx[k * P - EMB_ROWS : (k + 1) * P - EMB_ROWS, :])
+            input_parts.append((weights, xin))
+
+        windows = [held.tile([P, SLOTS], F32, name=f"window{c}") for c in range(BLOCKS)]
+        nc.sync.dma_start(windows[0][:], base[0:P, :])
+        nc.scalar.dma_start(windows[1][:], base[P : 2 * P, :])
+
+        bias_ih = held.tile([P, 3 * BLOCKS], F32, name="bias_ih")
+        bias_hh = held.tile([P, 3 * BLOCKS], F32, name="bias_hh")
+        with nc.allow_non_contiguous_dma(reason="768 biases, one to a partition"):
+            nc.gpsimd.dma_start(bias_ih[:], b_ih.rearrange("(g p) o -> p (g o)", p=P))
+            nc.gpsimd.dma_start(bias_hh[:], b_hh.rearrange("(g p) o -> p (g o)", p=P))
+        bias_sum = held.tile([P, 3 * BLOCKS], F32, name="bias_sum")
+        bias_neg = held.tile([P, 3 * BLOCKS], F32, name="bias_neg")
+        nc.vector.tensor_tensor(bias_sum[:], bias_ih[:], bias_hh[:], ADD)
+        nc.vector.tensor_scalar_mul(bias_neg[:], bias_sum[:], -1.0)
+
+        for c in range(BLOCKS):
+            fresh = work.tile([P, STREAMS], F32, name="fresh")
+            kept = work.tile([P, STREAMS], F32, name="kept")
+            col_r, col_z, col_n = (slice(BLOCKS * g + c, BLOCKS * g + c + 1) for g in (R, Z, N))
+            for half in range(STREAMS // BANK):
+                streams = slice(half * BANK, (half + 1) * BANK)
+                w_r, w_z, w_n = (
+                    slice(g * CHANNELS + c * P, g * CHANNELS + (c + 1) * P) for g in (R, Z, N)
+                )
+
+                ps_vn = psum.tile([P, BANK], F32, name="ps_vn")
+                ps_r = psum.tile([P, BANK], F32, name="ps_r")
+                ps_z = psum.tile([P, BANK], F32, name="ps_z")
+                ps_un = psum.tile([P, BANK], F32, name="ps_un")
+                accumulate(nc, ps_vn, hidden_parts, w_n, streams)
+                accumulate(nc, ps_r, hidden_parts + input_parts, w_r, streams)
+                accumulate(nc, ps_z, hidden_parts + input_parts, w_z, streams)
+                accumulate(nc, ps_un, input_parts, w_n, streams)
+
+                r = work.tile([P, BANK], F32, name="r")
+                nc.scalar.activation(r[:], ps_r[:], SIGMOID, bias=bias_sum[:, col_r])
+                r_vn = work.tile([P, BANK], F32, name="r_vn")
+                nc.vector.scalar_tensor_tensor(r_vn[:], ps_vn[:], bias_hh[:, col_n], r[:], ADD, MULT)
+
+                z = work.tile([P, BANK], F32, name="z")
+                one_minus_z = work.tile([P, BANK], F32, name="one_minus_z")
+                nc.scalar.activation(z[:], ps_z[:], SIGMOID, bias=bias_sum[:, col_z])
+                nc.scalar.activation(
+                    one_minus_z[:], ps_z[:], SIGMOID, bias=bias_neg[:, col_z], scale=-1.0
+                )
+                nc.vector.tensor_tensor(kept[:, streams], z[:], hidden_parts[c][1][:, streams], MULT)
+
+                pre_n = work.tile([P, BANK], F32, name="pre_n")
+                n = work.tile([P, BANK], F32, name="n")
+                nc.vector.tensor_tensor(pre_n[:], r_vn[:], ps_un[:], ADD)
+                nc.scalar.activation(n[:], pre_n[:], TANH, bias=bias_ih[:, col_n])
+                nc.vector.tensor_tensor(fresh[:, streams], one_minus_z[:], n[:], MULT)
+
+            nc.vector.tensor_tensor(windows[c][:].indirect(offsets[:]), fresh[:], kept[:], ADD)
+            nc.sync.dma_start(out[c * P : (c + 1) * P, :], windows[c][:])

@@ -1,4 +1,5 @@
 import concourse.mybir as mybir
+from concourse.masks import make_identity
 
 F32 = mybir.dt.float32
 BF16 = mybir.dt.bfloat16
@@ -11,24 +12,23 @@ TANH = mybir.ActivationFunctionType.Tanh
 P = 128
 CHANNELS = 256
 BLOCKS = CHANNELS // P
-EMB_ROWS = 256
-IN_ROWS = 768
 STREAMS = 1024
 SLOTS = 4096
 BANK = 512
+HALVES = STREAMS // BANK
 R, Z, N = 0, 1, 2
 
-FLOPS = 2 * STREAMS * 3 * CHANNELS * (IN_ROWS + CHANNELS)
+FLOPS = 2 * STREAMS * 3 * CHANNELS * (768 + CHANNELS)
 
 
-def accumulate(nc, bank, parts, gate_columns, streams):
-    for i, (weights, activations) in enumerate(parts):
+def accumulate(nc, bank, slabs, gate_columns):
+    for i, (weights, activations) in enumerate(slabs):
         nc.tensor.matmul(
             bank[:],
             weights[:, gate_columns],
-            activations[:, streams],
+            activations,
             start=(i == 0),
-            stop=(i == len(parts) - 1),
+            stop=(i == len(slabs) - 1),
         )
 
 
@@ -39,80 +39,91 @@ def tile_rnndecoder_kernel(tc, base, emb, ctx, h, w_ih, w_hh, b_ih, b_hh, offs, 
         tc.tile_pool(name="work", bufs=2) as work,
         tc.psum_pool(name="psum", bufs=2) as psum,
     ):
+        pairs = [
+            (w_hh, h),
+            (w_ih[0:256, :], emb),
+            (w_ih[256:512, :], ctx[0:256, :]),
+            (w_ih[512:768, :], ctx[256:512, :]),
+        ]
+        weight_tiles = []
+        stream_tiles = [[], []]
+        for d, (w_rows, x_rows) in enumerate(pairs):
+            weights = held.tile([P, 2, 3 * CHANNELS], BF16, name=f"weights{d}")
+            first = held.tile([P, 2, BANK], BF16, name=f"streams{d}_0")
+            nc.sync.dma_start(weights[:], w_rows.rearrange("(k p) m -> p k m", p=P))
+            nc.scalar.dma_start(first[:], x_rows.rearrange("(k p) n -> p k n", p=P)[:, :, 0:BANK])
+            weight_tiles.append(weights)
+            stream_tiles[0].append(first)
+        for d, (w_rows, x_rows) in enumerate(pairs):
+            second = held.tile([P, 2, BANK], BF16, name=f"streams{d}_1")
+            nc.scalar.dma_start(second[:], x_rows.rearrange("(k p) n -> p k n", p=P)[:, :, BANK:STREAMS])
+            stream_tiles[1].append(second)
+
+        bias_rows = held.tile([P, P], F32, name="bias_rows")
+        nc.gpsimd.memset(bias_rows[:], 0.0)
+        nc.sync.dma_start(bias_rows[0 : 3 * BLOCKS, :], b_ih.rearrange("(g p) o -> g (p o)", p=P))
+        nc.sync.dma_start(bias_rows[3 * BLOCKS : 6 * BLOCKS, :], b_hh.rearrange("(g p) o -> g (p o)", p=P))
+
         offsets = held.tile([P, STREAMS // 16], U16, name="offsets")
         nc.sync.dma_start(offsets[:], offs)
-
-        hidden_parts = []
-        for k in range(CHANNELS // P):
-            rows = slice(k * P, (k + 1) * P)
-            weights = held.tile([P, 3 * CHANNELS], BF16, name=f"w_hh{k}")
-            hidden = held.tile([P, STREAMS], BF16, name=f"h{k}")
-            nc.sync.dma_start(weights[:], w_hh[rows, :])
-            nc.scalar.dma_start(hidden[:], h[rows, :])
-            hidden_parts.append((weights, hidden))
-        input_parts = []
-        for k in range(IN_ROWS // P):
-            rows = slice(k * P, (k + 1) * P)
-            weights = held.tile([P, 3 * CHANNELS], BF16, name=f"w_ih{k}")
-            xin = held.tile([P, STREAMS], BF16, name=f"xin{k}")
-            nc.sync.dma_start(weights[:], w_ih[rows, :])
-            if k * P < EMB_ROWS:
-                nc.scalar.dma_start(xin[:], emb[rows, :])
-            else:
-                nc.scalar.dma_start(xin[:], ctx[k * P - EMB_ROWS : (k + 1) * P - EMB_ROWS, :])
-            input_parts.append((weights, xin))
 
         windows = [held.tile([P, SLOTS], F32, name=f"window{c}") for c in range(BLOCKS)]
         nc.sync.dma_start(windows[0][:], base[0:P, :])
         nc.scalar.dma_start(windows[1][:], base[P : 2 * P, :])
 
-        bias_ih = held.tile([P, 3 * BLOCKS], F32, name="bias_ih")
-        bias_hh = held.tile([P, 3 * BLOCKS], F32, name="bias_hh")
-        with nc.allow_non_contiguous_dma(reason="768 biases, one to a partition"):
-            nc.gpsimd.dma_start(bias_ih[:], b_ih.rearrange("(g p) o -> p (g o)", p=P))
-            nc.gpsimd.dma_start(bias_hh[:], b_hh.rearrange("(g p) o -> p (g o)", p=P))
+        identity = held.tile([P, P], F32, name="identity")
+        make_identity(nc, identity[:])
+        ps_bias = psum.tile([P, P], F32, name="ps_bias", tag="ps_un")
+        nc.tensor.transpose(ps_bias[:], bias_rows[:], identity[:])
+        bias_columns = held.tile([P, 6 * BLOCKS], F32, name="bias_columns")
+        nc.vector.tensor_copy(bias_columns[:], ps_bias[:, 0 : 6 * BLOCKS])
+        bias_ih = bias_columns[:, 0 : 3 * BLOCKS]
+        bias_hh = bias_columns[:, 3 * BLOCKS : 6 * BLOCKS]
         bias_sum = held.tile([P, 3 * BLOCKS], F32, name="bias_sum")
         bias_neg = held.tile([P, 3 * BLOCKS], F32, name="bias_neg")
-        nc.vector.tensor_tensor(bias_sum[:], bias_ih[:], bias_hh[:], ADD)
+        nc.vector.tensor_tensor(bias_sum[:], bias_ih, bias_hh, ADD)
         nc.vector.tensor_scalar_mul(bias_neg[:], bias_sum[:], -1.0)
 
         for c in range(BLOCKS):
             fresh = work.tile([P, STREAMS], F32, name="fresh")
             kept = work.tile([P, STREAMS], F32, name="kept")
             col_r, col_z, col_n = (slice(BLOCKS * g + c, BLOCKS * g + c + 1) for g in (R, Z, N))
-            for half in range(STREAMS // BANK):
+            w_r, w_z, w_n = (slice(g * CHANNELS + c * P, g * CHANNELS + (c + 1) * P) for g in (R, Z, N))
+            for half in range(HALVES):
                 streams = slice(half * BANK, (half + 1) * BANK)
-                w_r, w_z, w_n = (
-                    slice(g * CHANNELS + c * P, g * CHANNELS + (c + 1) * P) for g in (R, Z, N)
-                )
+                slabs = [
+                    (weight_tiles[d][:, k, :], stream_tiles[half][d][:, k, :])
+                    for d in range(len(pairs))
+                    for k in range(2)
+                ]
+                hidden_slabs, input_slabs = slabs[0:2], slabs[2:]
 
                 ps_vn = psum.tile([P, BANK], F32, name="ps_vn")
                 ps_r = psum.tile([P, BANK], F32, name="ps_r")
                 ps_z = psum.tile([P, BANK], F32, name="ps_z")
                 ps_un = psum.tile([P, BANK], F32, name="ps_un")
-                accumulate(nc, ps_vn, hidden_parts, w_n, streams)
-                accumulate(nc, ps_r, hidden_parts + input_parts, w_r, streams)
-                accumulate(nc, ps_z, hidden_parts + input_parts, w_z, streams)
-                accumulate(nc, ps_un, input_parts, w_n, streams)
+                accumulate(nc, ps_vn, hidden_slabs, w_n)
+                accumulate(nc, ps_r, slabs, w_r)
+                accumulate(nc, ps_un, input_slabs, w_n)
+                accumulate(nc, ps_z, slabs, w_z)
 
                 r = work.tile([P, BANK], F32, name="r")
-                nc.scalar.activation(r[:], ps_r[:], SIGMOID, bias=bias_sum[:, col_r])
                 r_vn = work.tile([P, BANK], F32, name="r_vn")
+                pre_n = work.tile([P, BANK], F32, name="pre_n")
+                n = work.tile([P, BANK], F32, name="n")
+                nc.scalar.activation(r[:], ps_r[:], SIGMOID, bias=bias_sum[:, col_r])
                 nc.vector.scalar_tensor_tensor(r_vn[:], ps_vn[:], bias_hh[:, col_n], r[:], ADD, MULT)
+                nc.vector.tensor_tensor(pre_n[:], r_vn[:], ps_un[:], ADD)
+                nc.scalar.activation(n[:], pre_n[:], TANH, bias=bias_ih[:, col_n])
 
-                z = work.tile([P, BANK], F32, name="z")
                 one_minus_z = work.tile([P, BANK], F32, name="one_minus_z")
-                nc.scalar.activation(z[:], ps_z[:], SIGMOID, bias=bias_sum[:, col_z])
+                z = work.tile([P, BANK], F32, name="z")
                 nc.scalar.activation(
                     one_minus_z[:], ps_z[:], SIGMOID, bias=bias_neg[:, col_z], scale=-1.0
                 )
-                nc.vector.tensor_tensor(kept[:, streams], z[:], hidden_parts[c][1][:, streams], MULT)
-
-                pre_n = work.tile([P, BANK], F32, name="pre_n")
-                n = work.tile([P, BANK], F32, name="n")
-                nc.vector.tensor_tensor(pre_n[:], r_vn[:], ps_un[:], ADD)
-                nc.scalar.activation(n[:], pre_n[:], TANH, bias=bias_ih[:, col_n])
+                nc.scalar.activation(z[:], ps_z[:], SIGMOID, bias=bias_sum[:, col_z])
                 nc.vector.tensor_tensor(fresh[:, streams], one_minus_z[:], n[:], MULT)
+                nc.vector.tensor_tensor(kept[:, streams], z[:], stream_tiles[half][0][:, c, :], MULT)
 
             nc.vector.tensor_tensor(windows[c][:].indirect(offsets[:]), fresh[:], kept[:], ADD)
             nc.sync.dma_start(out[c * P : (c + 1) * P, :], windows[c][:])

@@ -17,6 +17,7 @@ SLOTS = 4096
 BANK = 512
 HALVES = STREAMS // BANK
 R, Z, N = 0, 1, 2
+WARM_UP_MATMULS = 6
 
 FLOPS = 2 * STREAMS * 3 * CHANNELS * (768 + CHANNELS)
 
@@ -39,6 +40,12 @@ def tile_rnndecoder_kernel(tc, base, emb, ctx, h, w_ih, w_hh, b_ih, b_hh, offs, 
         tc.tile_pool(name="work", bufs=2) as work,
         tc.psum_pool(name="psum", bufs=2) as psum,
     ):
+        zeros = held.tile([P, BANK], BF16, name="zeros")
+        nc.vector.memset(zeros[:], 0.0)
+        ps_start = psum.tile([P, BANK], F32, name="ps_start", tag="ps_un")
+        for i in range(WARM_UP_MATMULS):
+            nc.tensor.matmul(ps_start[:], zeros[:, 0:P], zeros[:], start=True, stop=True)
+
         pairs = [
             (w_hh, h),
             (w_ih[0:256, :], emb),
@@ -73,10 +80,9 @@ def tile_rnndecoder_kernel(tc, base, emb, ctx, h, w_ih, w_hh, b_ih, b_hh, offs, 
 
         identity = held.tile([P, P], F32, name="identity")
         make_identity(nc, identity[:])
-        ps_bias = psum.tile([P, P], F32, name="ps_bias", tag="ps_un")
-        nc.tensor.transpose(ps_bias[:], bias_rows[:], identity[:])
+        nc.tensor.transpose(ps_start[:, 0:P], bias_rows[:], identity[:])
         bias_columns = held.tile([P, 6 * BLOCKS], F32, name="bias_columns")
-        nc.vector.tensor_copy(bias_columns[:], ps_bias[:, 0 : 6 * BLOCKS])
+        nc.vector.tensor_copy(bias_columns[:], ps_start[:, 0 : 6 * BLOCKS])
         bias_ih = bias_columns[:, 0 : 3 * BLOCKS]
         bias_hh = bias_columns[:, 3 * BLOCKS : 6 * BLOCKS]
         bias_sum = held.tile([P, 3 * BLOCKS], F32, name="bias_sum")
@@ -104,26 +110,27 @@ def tile_rnndecoder_kernel(tc, base, emb, ctx, h, w_ih, w_hh, b_ih, b_hh, offs, 
                 ps_un = psum.tile([P, BANK], F32, name="ps_un")
                 accumulate(nc, ps_vn, hidden_slabs, w_n)
                 accumulate(nc, ps_r, slabs, w_r)
-                accumulate(nc, ps_un, input_slabs, w_n)
                 accumulate(nc, ps_z, slabs, w_z)
+                accumulate(nc, ps_un, input_slabs, w_n)
 
                 r = work.tile([P, BANK], F32, name="r")
-                r_vn = work.tile([P, BANK], F32, name="r_vn")
-                pre_n = work.tile([P, BANK], F32, name="pre_n")
-                n = work.tile([P, BANK], F32, name="n")
                 nc.scalar.activation(r[:], ps_r[:], SIGMOID, bias=bias_sum[:, col_r])
+                r_vn = work.tile([P, BANK], F32, name="r_vn")
                 nc.vector.scalar_tensor_tensor(r_vn[:], ps_vn[:], bias_hh[:, col_n], r[:], ADD, MULT)
-                nc.vector.tensor_tensor(pre_n[:], r_vn[:], ps_un[:], ADD)
-                nc.scalar.activation(n[:], pre_n[:], TANH, bias=bias_ih[:, col_n])
 
-                one_minus_z = work.tile([P, BANK], F32, name="one_minus_z")
                 z = work.tile([P, BANK], F32, name="z")
+                one_minus_z = work.tile([P, BANK], F32, name="one_minus_z")
+                nc.scalar.activation(z[:], ps_z[:], SIGMOID, bias=bias_sum[:, col_z])
                 nc.scalar.activation(
                     one_minus_z[:], ps_z[:], SIGMOID, bias=bias_neg[:, col_z], scale=-1.0
                 )
-                nc.scalar.activation(z[:], ps_z[:], SIGMOID, bias=bias_sum[:, col_z])
-                nc.vector.tensor_tensor(fresh[:, streams], one_minus_z[:], n[:], MULT)
                 nc.vector.tensor_tensor(kept[:, streams], z[:], stream_tiles[half][0][:, c, :], MULT)
+
+                pre_n = work.tile([P, BANK], F32, name="pre_n")
+                n = work.tile([P, BANK], F32, name="n")
+                nc.vector.tensor_tensor(pre_n[:], r_vn[:], ps_un[:], ADD)
+                nc.scalar.activation(n[:], pre_n[:], TANH, bias=bias_ih[:, col_n])
+                nc.vector.tensor_tensor(fresh[:, streams], one_minus_z[:], n[:], MULT)
 
             nc.vector.tensor_tensor(windows[c][:].indirect(offsets[:]), fresh[:], kept[:], ADD)
             nc.sync.dma_start(out[c * P : (c + 1) * P, :], windows[c][:])

@@ -22,17 +22,6 @@ WARM_UP_MATMULS = 6
 FLOPS = 2 * STREAMS * 3 * CHANNELS * (768 + CHANNELS)
 
 
-def accumulate(nc, bank, slabs, gate_columns):
-    for i, (weights, activations) in enumerate(slabs):
-        nc.tensor.matmul(
-            bank[:],
-            weights[:, gate_columns],
-            activations,
-            start=(i == 0),
-            stop=(i == len(slabs) - 1),
-        )
-
-
 def tile_rnndecoder_kernel(tc, base, emb, ctx, h, w_ih, w_hh, b_ih, b_hh, offs, out):
     nc = tc.nc
     with (
@@ -102,16 +91,24 @@ def tile_rnndecoder_kernel(tc, base, emb, ctx, h, w_ih, w_hh, b_ih, b_hh, offs, 
                     for d in range(len(pairs))
                     for k in range(2)
                 ]
-                hidden_slabs, input_slabs = slabs[0:2], slabs[2:]
 
                 ps_vn = psum.tile([P, BANK], F32, name="ps_vn")
                 ps_r = psum.tile([P, BANK], F32, name="ps_r")
                 ps_z = psum.tile([P, BANK], F32, name="ps_z")
                 ps_un = psum.tile([P, BANK], F32, name="ps_un")
-                accumulate(nc, ps_vn, hidden_slabs, w_n)
-                accumulate(nc, ps_r, slabs, w_r)
-                accumulate(nc, ps_z, slabs, w_z)
-                accumulate(nc, ps_un, input_slabs, w_n)
+                products = [(ps_vn, w_n, 0, 2), (ps_r, w_r, 0, 8), (ps_z, w_z, 0, 8), (ps_un, w_n, 2, 8)]
+                steps = [
+                    (s, bank, gate_columns, s == begin, s == end - 1)
+                    for bank, gate_columns, begin, end in products
+                    for s in range(begin, end)
+                ]
+                if c == 0 and half == 0:
+                    steps = sorted(steps, key=lambda step: step[0])
+                for s, bank, gate_columns, is_first, is_last in steps:
+                    weights, activations = slabs[s]
+                    nc.tensor.matmul(
+                        bank[:], weights[:, gate_columns], activations, start=is_first, stop=is_last
+                    )
 
                 r = work.tile([P, BANK], F32, name="r")
                 nc.scalar.activation(r[:], ps_r[:], SIGMOID, bias=bias_sum[:, col_r])

@@ -17,7 +17,7 @@ SLOTS = 4096
 BANK = 512
 HALVES = STREAMS // BANK
 R, Z, N = 0, 1, 2
-WARM_UP_MATMULS = 6
+WARM_UP_MATMULS = 4
 
 FLOPS = 2 * STREAMS * 3 * CHANNELS * (768 + CHANNELS)
 

@@ -36,24 +36,27 @@ def tile_rnndecoder_kernel(tc, base, emb, ctx, h, w_ih, w_hh, b_ih, b_hh, offs, 
             nc.tensor.matmul(ps_start[:], zeros[:, 0:P], zeros[:], start=True, stop=True)
 
         pairs = [
-            (w_hh, h),
+            (w_hh[0:128, :], h[0:128, :]),
+            (w_hh[128:256, :], h[128:256, :]),
             (w_ih[0:256, :], emb),
             (w_ih[256:512, :], ctx[0:256, :]),
             (w_ih[512:768, :], ctx[256:512, :]),
         ]
+        slabs = [[], []]
         weight_tiles = []
-        stream_tiles = [[], []]
         for d, (w_rows, x_rows) in enumerate(pairs):
-            weights = held.tile([P, 2, 3 * CHANNELS], BF16, name=f"weights{d}")
-            first = held.tile([P, 2, BANK], BF16, name=f"streams{d}_0")
+            count = w_rows.shape[0] // P
+            weights = held.tile([P, count, 3 * CHANNELS], BF16, name=f"weights{d}")
+            first = held.tile([P, count, BANK], BF16, name=f"streams{d}_0")
             nc.sync.dma_start(weights[:], w_rows.rearrange("(k p) m -> p k m", p=P))
             nc.scalar.dma_start(first[:], x_rows.rearrange("(k p) n -> p k n", p=P)[:, :, 0:BANK])
             weight_tiles.append(weights)
-            stream_tiles[0].append(first)
+            slabs[0] += [(weights[:, k, :], first[:, k, :]) for k in range(count)]
         for d, (w_rows, x_rows) in enumerate(pairs):
-            second = held.tile([P, 2, BANK], BF16, name=f"streams{d}_1")
+            count = w_rows.shape[0] // P
+            second = held.tile([P, count, BANK], BF16, name=f"streams{d}_1")
             nc.scalar.dma_start(second[:], x_rows.rearrange("(k p) n -> p k n", p=P)[:, :, BANK:STREAMS])
-            stream_tiles[1].append(second)
+            slabs[1] += [(weight_tiles[d][:, k, :], second[:, k, :]) for k in range(count)]
 
         bias_rows = held.tile([P, P], F32, name="bias_rows")
         nc.gpsimd.memset(bias_rows[:], 0.0)
@@ -86,11 +89,6 @@ def tile_rnndecoder_kernel(tc, base, emb, ctx, h, w_ih, w_hh, b_ih, b_hh, offs, 
             w_r, w_z, w_n = (slice(g * CHANNELS + c * P, g * CHANNELS + (c + 1) * P) for g in (R, Z, N))
             for half in range(HALVES):
                 streams = slice(half * BANK, (half + 1) * BANK)
-                slabs = [
-                    (weight_tiles[d][:, k, :], stream_tiles[half][d][:, k, :])
-                    for d in range(len(pairs))
-                    for k in range(2)
-                ]
 
                 ps_vn = psum.tile([P, BANK], F32, name="ps_vn")
                 ps_r = psum.tile([P, BANK], F32, name="ps_r")
@@ -105,7 +103,7 @@ def tile_rnndecoder_kernel(tc, base, emb, ctx, h, w_ih, w_hh, b_ih, b_hh, offs, 
                 if c == 0 and half == 0:
                     steps = sorted(steps, key=lambda step: step[0])
                 for s, bank, gate_columns, is_first, is_last in steps:
-                    weights, activations = slabs[s]
+                    weights, activations = slabs[half][s]
                     nc.tensor.matmul(
                         bank[:], weights[:, gate_columns], activations, start=is_first, stop=is_last
                     )
@@ -121,7 +119,7 @@ def tile_rnndecoder_kernel(tc, base, emb, ctx, h, w_ih, w_hh, b_ih, b_hh, offs, 
                 nc.scalar.activation(
                     one_minus_z[:], ps_z[:], SIGMOID, bias=bias_neg[:, col_z], scale=-1.0
                 )
-                nc.vector.tensor_tensor(kept[:, streams], z[:], stream_tiles[half][0][:, c, :], MULT)
+                nc.vector.tensor_tensor(kept[:, streams], z[:], slabs[half][c][1], MULT)
 
                 pre_n = work.tile([P, BANK], F32, name="pre_n")
                 n = work.tile([P, BANK], F32, name="n")

@@ -119,7 +119,7 @@ def tile_rnndecoder_kernel(tc, base, emb, ctx, h, w_ih, w_hh, b_ih, b_hh, offs, 
                 nc.scalar.activation(
                     one_minus_z[:], ps_z[:], SIGMOID, bias=bias_neg[:, col_z], scale=-1.0
                 )
-                nc.vector.tensor_tensor(kept[:, streams], z[:], slabs[half][c][1], MULT)
+                nc.gpsimd.tensor_tensor(kept[:, streams], z[:], slabs[half][c][1], MULT)
 
                 pre_n = work.tile([P, BANK], F32, name="pre_n")
                 n = work.tile([P, BANK], F32, name="n")

@@ -16,6 +16,7 @@ STREAMS = 1024
 SLOTS = 4096
 BANK = 512
 HALVES = STREAMS // BANK
+PSUM_BANKS = 8
 R, Z, N = 0, 1, 2
 WARM_UP_MATMULS = 4
 
@@ -27,11 +28,11 @@ def tile_rnndecoder_kernel(tc, base, emb, ctx, h, w_ih, w_hh, b_ih, b_hh, offs, 
     with (
         tc.tile_pool(name="held", bufs=1) as held,
         tc.tile_pool(name="work", bufs=2) as work,
-        tc.psum_pool(name="psum", bufs=2) as psum,
+        tc.psum_pool(name="psum", bufs=PSUM_BANKS) as psum,
     ):
         zeros = held.tile([P, BANK], BF16, name="zeros")
         nc.vector.memset(zeros[:], 0.0)
-        ps_start = psum.tile([P, BANK], F32, name="ps_start", tag="ps_un")
+        ps_start = psum.tile([P, BANK], F32, name="ps_start", tag="product")
         for i in range(WARM_UP_MATMULS):
             nc.tensor.matmul(ps_start[:], zeros[:, 0:P], zeros[:], start=True, stop=True)
 
@@ -82,50 +83,95 @@ def tile_rnndecoder_kernel(tc, base, emb, ctx, h, w_ih, w_hh, b_ih, b_hh, offs, 
         nc.vector.tensor_tensor(bias_sum[:], bias_ih, bias_hh, ADD)
         nc.vector.tensor_scalar_mul(bias_neg[:], bias_sum[:], -1.0)
 
-        for c in range(BLOCKS):
-            fresh = work.tile([P, STREAMS], F32, name="fresh")
-            kept = work.tile([P, STREAMS], F32, name="kept")
-            col_r, col_z, col_n = (slice(BLOCKS * g + c, BLOCKS * g + c + 1) for g in (R, Z, N))
-            w_r, w_z, w_n = (slice(g * CHANNELS + c * P, g * CHANNELS + (c + 1) * P) for g in (R, Z, N))
-            for half in range(HALVES):
-                streams = slice(half * BANK, (half + 1) * BANK)
-
-                ps_vn = psum.tile([P, BANK], F32, name="ps_vn")
-                ps_r = psum.tile([P, BANK], F32, name="ps_r")
-                ps_z = psum.tile([P, BANK], F32, name="ps_z")
-                ps_un = psum.tile([P, BANK], F32, name="ps_un")
-                products = [(ps_vn, w_n, 0, 2), (ps_r, w_r, 0, 8), (ps_z, w_z, 0, 8), (ps_un, w_n, 2, 8)]
-                steps = [
-                    (s, bank, gate_columns, s == begin, s == end - 1)
-                    for bank, gate_columns, begin, end in products
-                    for s in range(begin, end)
-                ]
-                if c == 0 and half == 0:
-                    steps = sorted(steps, key=lambda step: step[0])
-                for s, bank, gate_columns, is_first, is_last in steps:
-                    weights, activations = slabs[half][s]
-                    nc.tensor.matmul(
-                        bank[:], weights[:, gate_columns], activations, start=is_first, stop=is_last
-                    )
-
-                r = work.tile([P, BANK], F32, name="r")
-                nc.scalar.activation(r[:], ps_r[:], SIGMOID, bias=bias_sum[:, col_r])
-                r_vn = work.tile([P, BANK], F32, name="r_vn")
-                nc.vector.scalar_tensor_tensor(r_vn[:], ps_vn[:], bias_hh[:, col_n], r[:], ADD, MULT)
-
-                z = work.tile([P, BANK], F32, name="z")
-                one_minus_z = work.tile([P, BANK], F32, name="one_minus_z")
-                nc.scalar.activation(z[:], ps_z[:], SIGMOID, bias=bias_sum[:, col_z])
-                nc.scalar.activation(
-                    one_minus_z[:], ps_z[:], SIGMOID, bias=bias_neg[:, col_z], scale=-1.0
+        def multiply(products, half, columns=slice(0, BANK), by_slab=False):
+            steps = [
+                (s, bank, gate_columns, s == begin, s == end - 1)
+                for bank, gate_columns, begin, end in products
+                for s in range(begin, end)
+            ]
+            if by_slab:
+                steps = sorted(steps, key=lambda step: step[0])
+            for s, bank, gate_columns, is_first, is_last in steps:
+                weights, activations = slabs[half][s]
+                nc.tensor.matmul(
+                    bank[:], weights[:, gate_columns], activations[:, columns], start=is_first, stop=is_last
                 )
-                nc.gpsimd.tensor_tensor(kept[:, streams], z[:], slabs[half][c][1], MULT)
 
-                pre_n = work.tile([P, BANK], F32, name="pre_n")
-                n = work.tile([P, BANK], F32, name="n")
-                nc.vector.tensor_tensor(pre_n[:], r_vn[:], ps_un[:], ADD)
-                nc.scalar.activation(n[:], pre_n[:], TANH, bias=bias_ih[:, col_n])
-                nc.vector.tensor_tensor(fresh[:, streams], one_minus_z[:], n[:], MULT)
+        def gates_r_z(c, half, ps_r, ps_z, kept):
+            col_r, col_z = (slice(BLOCKS * g + c, BLOCKS * g + c + 1) for g in (R, Z))
+            r = work.tile([P, BANK], F32, name="r")
+            z = work.tile([P, BANK], F32, name="z")
+            one_minus_z = work.tile([P, BANK], F32, name="one_minus_z")
+            nc.scalar.activation(r[:], ps_r[:], SIGMOID, bias=bias_sum[:, col_r])
+            nc.scalar.activation(z[:], ps_z[:], SIGMOID, bias=bias_sum[:, col_z])
+            nc.scalar.activation(one_minus_z[:], ps_z[:], SIGMOID, bias=bias_neg[:, col_z], scale=-1.0)
+            nc.gpsimd.tensor_tensor(kept[:, half * BANK : (half + 1) * BANK], z[:], slabs[half][c][1], MULT)
+            return r, one_minus_z
 
+        def reset_v_n(c, ps_vn, r):
+            r_vn = work.tile([P, BANK], F32, name="r_vn")
+            nc.vector.scalar_tensor_tensor(
+                r_vn[:], ps_vn[:], bias_hh[:, BLOCKS * N + c : BLOCKS * N + c + 1], r[:], ADD, MULT
+            )
+            return r_vn
+
+        def gate_n(c, half, columns, ps_un, r_vn, one_minus_z, fresh):
+            width = columns.stop - columns.start
+            pre_n = work.tile([P, width], F32, name="pre_n")
+            n = work.tile([P, width], F32, name="n")
+            nc.vector.tensor_tensor(pre_n[:], r_vn[:, columns], ps_un[:], ADD)
+            nc.scalar.activation(n[:], pre_n[:], TANH, bias=bias_ih[:, BLOCKS * N + c : BLOCKS * N + c + 1])
+            nc.vector.tensor_tensor(
+                fresh[:, half * BANK + columns.start : half * BANK + columns.stop], one_minus_z[:, columns], n[:], MULT
+            )
+
+        def scatter(c, fresh, kept):
             nc.vector.tensor_tensor(windows[c][:].indirect(offsets[:]), fresh[:], kept[:], ADD)
             nc.sync.dma_start(out[c * P : (c + 1) * P, :], windows[c][:])
+
+        def gate_columns_of(c):
+            return (slice(g * CHANNELS + c * P, g * CHANNELS + (c + 1) * P) for g in (R, Z, N))
+
+        def new_bank(width=BANK):
+            return psum.tile([P, width], F32, name="product")
+
+
+        c = 0
+        w_r, w_z, w_n = gate_columns_of(c)
+        fresh = work.tile([P, STREAMS], F32, name="fresh")
+        kept = work.tile([P, STREAMS], F32, name="kept")
+        for half in range(HALVES):
+            ps_vn, ps_r, ps_z, ps_un = new_bank(), new_bank(), new_bank(), new_bank()
+            multiply(
+                [(ps_vn, w_n, 0, 2), (ps_r, w_r, 0, 8), (ps_z, w_z, 0, 8), (ps_un, w_n, 2, 8)],
+                half,
+                by_slab=half == 0,
+            )
+            r, one_minus_z = gates_r_z(c, half, ps_r, ps_z, kept)
+            r_vn = reset_v_n(c, ps_vn, r)
+            gate_n(c, half, slice(0, BANK), ps_un, r_vn, one_minus_z, fresh)
+        scatter(c, fresh, kept)
+
+        c = 1
+        w_r, w_z, w_n = gate_columns_of(c)
+        fresh = work.tile([P, STREAMS], F32, name="fresh")
+        kept = work.tile([P, STREAMS], F32, name="kept")
+        gates = []
+        for half in range(HALVES):
+            ps_r, ps_z = new_bank(), new_bank()
+            multiply([(ps_r, w_r, 0, 8), (ps_z, w_z, 0, 8)], half)
+            gates.append(gates_r_z(c, half, ps_r, ps_z, kept))
+        pieces = [[BANK], [BANK // 2, BANK // 2]]
+        for half in range(HALVES):
+            r, one_minus_z = gates[half]
+            ps_vn = new_bank()
+            multiply([(ps_vn, w_n, 0, 2)], half)
+            r_vn = reset_v_n(c, ps_vn, r)
+            left = 0
+            for width in pieces[half]:
+                columns = slice(left, left + width)
+                ps_un = new_bank(width)
+                multiply([(ps_un, w_n, 2, 8)], half, columns)
+                gate_n(c, half, columns, ps_un, r_vn, one_minus_z, fresh)
+                left += width
+        scatter(c, fresh, kept)

@@ -43,33 +43,37 @@ def tile_rnndecoder_kernel(tc, base, emb, ctx, h, w_ih, w_hh, b_ih, b_hh, offs, 
             (w_ih[256:512, :], ctx[0:256, :]),
             (w_ih[512:768, :], ctx[256:512, :]),
         ]
+        queues = [nc.sync, nc.scalar]
         slabs = [[], []]
         weight_tiles = []
         for d, (w_rows, x_rows) in enumerate(pairs):
             count = w_rows.shape[0] // P
             weights = held.tile([P, count, 3 * CHANNELS], BF16, name=f"weights{d}")
             first = held.tile([P, count, BANK], BF16, name=f"streams{d}_0")
-            nc.sync.dma_start(weights[:], w_rows.rearrange("(k p) m -> p k m", p=P))
-            nc.scalar.dma_start(first[:], x_rows.rearrange("(k p) n -> p k n", p=P)[:, :, 0:BANK])
+            queues[d % 2].dma_start(weights[:], w_rows.rearrange("(k p) m -> p k m", p=P))
+            queues[(d + 1) % 2].dma_start(first[:], x_rows.rearrange("(k p) n -> p k n", p=P)[:, :, 0:BANK])
             weight_tiles.append(weights)
             slabs[0] += [(weights[:, k, :], first[:, k, :]) for k in range(count)]
-        for d, (w_rows, x_rows) in enumerate(pairs):
-            count = w_rows.shape[0] // P
-            second = held.tile([P, count, BANK], BF16, name=f"streams{d}_1")
-            nc.scalar.dma_start(second[:], x_rows.rearrange("(k p) n -> p k n", p=P)[:, :, BANK:STREAMS])
-            slabs[1] += [(weight_tiles[d][:, k, :], second[:, k, :]) for k in range(count)]
 
         bias_rows = held.tile([P, P], F32, name="bias_rows")
         nc.gpsimd.memset(bias_rows[:], 0.0)
         nc.sync.dma_start(bias_rows[0 : 3 * BLOCKS, :], b_ih.rearrange("(g p) o -> g (p o)", p=P))
-        nc.sync.dma_start(bias_rows[3 * BLOCKS : 6 * BLOCKS, :], b_hh.rearrange("(g p) o -> g (p o)", p=P))
+        nc.scalar.dma_start(bias_rows[3 * BLOCKS : 6 * BLOCKS, :], b_hh.rearrange("(g p) o -> g (p o)", p=P))
+
+        for d, (w_rows, x_rows) in enumerate(pairs):
+            count = w_rows.shape[0] // P
+            second = held.tile([P, count, BANK], BF16, name=f"streams{d}_1")
+            queues[(d + 1) % 2].dma_start(second[:], x_rows.rearrange("(k p) n -> p k n", p=P)[:, :, BANK:STREAMS])
+            slabs[1] += [(weight_tiles[d][:, k, :], second[:, k, :]) for k in range(count)]
 
         offsets = held.tile([P, STREAMS // 16], U16, name="offsets")
         nc.sync.dma_start(offsets[:], offs)
 
         windows = [held.tile([P, SLOTS], F32, name=f"window{c}") for c in range(BLOCKS)]
-        nc.sync.dma_start(windows[0][:], base[0:P, :])
-        nc.scalar.dma_start(windows[1][:], base[P : 2 * P, :])
+        for c in range(BLOCKS):
+            for q, queue in enumerate(queues):
+                columns = slice(q * SLOTS // 2, (q + 1) * SLOTS // 2)
+                queue.dma_start(windows[c][:, columns], base[c * P : (c + 1) * P, columns])
 
         identity = held.tile([P, P], F32, name="identity")
         make_identity(nc, identity[:])

@@ -139,43 +139,45 @@ def tile_rnndecoder_kernel(tc, base, emb, ctx, h, w_ih, w_hh, b_ih, b_hh, offs, 
         def new_bank(width=BANK):
             return psum.tile([P, width], F32, name="product")
 
-
-        c = 0
-        w_r, w_z, w_n = gate_columns_of(c)
-        fresh = work.tile([P, STREAMS], F32, name="fresh")
-        kept = work.tile([P, STREAMS], F32, name="kept")
-        for half in range(HALVES):
-            ps_vn, ps_r, ps_z, ps_un = new_bank(), new_bank(), new_bank(), new_bank()
-            multiply(
-                [(ps_vn, w_n, 0, 2), (ps_r, w_r, 0, 8), (ps_z, w_z, 0, 8), (ps_un, w_n, 2, 8)],
-                half,
-                by_slab=half == 0,
-            )
-            r, one_minus_z = gates_r_z(c, half, ps_r, ps_z, kept)
-            r_vn = reset_v_n(c, ps_vn, r)
-            gate_n(c, half, slice(0, BANK), ps_un, r_vn, one_minus_z, fresh)
-        scatter(c, fresh, kept)
-
-        c = 1
-        w_r, w_z, w_n = gate_columns_of(c)
-        fresh = work.tile([P, STREAMS], F32, name="fresh")
-        kept = work.tile([P, STREAMS], F32, name="kept")
-        gates = []
-        for half in range(HALVES):
+        def stage_r_z(c, half, kept):
+            w_r, w_z, w_n = gate_columns_of(c)
             ps_r, ps_z = new_bank(), new_bank()
             multiply([(ps_r, w_r, 0, 8), (ps_z, w_z, 0, 8)], half)
-            gates.append(gates_r_z(c, half, ps_r, ps_z, kept))
-        pieces = [[BANK], [BANK // 2, BANK // 2]]
-        for half in range(HALVES):
-            r, one_minus_z = gates[half]
+            return gates_r_z(c, half, ps_r, ps_z, kept)
+
+        def stage_n(c, half, widths, r, one_minus_z, fresh):
+            w_r, w_z, w_n = gate_columns_of(c)
             ps_vn = new_bank()
             multiply([(ps_vn, w_n, 0, 2)], half)
             r_vn = reset_v_n(c, ps_vn, r)
             left = 0
-            for width in pieces[half]:
+            for width in widths:
                 columns = slice(left, left + width)
                 ps_un = new_bank(width)
                 multiply([(ps_un, w_n, 2, 8)], half, columns)
                 gate_n(c, half, columns, ps_un, r_vn, one_minus_z, fresh)
                 left += width
+
+        whole, in_two = [BANK], [BANK // 2, BANK // 2]
+
+        c = 0
+        w_r, w_z, w_n = gate_columns_of(c)
+        fresh = work.tile([P, STREAMS], F32, name="fresh")
+        kept = work.tile([P, STREAMS], F32, name="kept")
+        ps_vn, ps_r, ps_z, ps_un = new_bank(), new_bank(), new_bank(), new_bank()
+        multiply([(ps_vn, w_n, 0, 2), (ps_r, w_r, 0, 8), (ps_z, w_z, 0, 8), (ps_un, w_n, 2, 8)], 0, by_slab=True)
+        r, one_minus_z = gates_r_z(c, 0, ps_r, ps_z, kept)
+        r_vn = reset_v_n(c, ps_vn, r)
+        gate_n(c, 0, slice(0, BANK), ps_un, r_vn, one_minus_z, fresh)
+        r, one_minus_z = stage_r_z(c, 1, kept)
+        stage_n(c, 1, in_two, r, one_minus_z, fresh)
+        scatter(c, fresh, kept)
+
+        c = 1
+        fresh = work.tile([P, STREAMS], F32, name="fresh")
+        kept = work.tile([P, STREAMS], F32, name="kept")
+        gates = [stage_r_z(c, half, kept) for half in range(HALVES)]
+        for half, widths in enumerate([whole, in_two]):
+            r, one_minus_z = gates[half]
+            stage_n(c, half, widths, r, one_minus_z, fresh)
         scatter(c, fresh, kept)

@@ -176,8 +176,7 @@ def tile_rnndecoder_kernel(tc, base, emb, ctx, h, w_ih, w_hh, b_ih, b_hh, offs, 
         c = 1
         fresh = work.tile([P, STREAMS], F32, name="fresh")
         kept = work.tile([P, STREAMS], F32, name="kept")
-        gates = [stage_r_z(c, half, kept) for half in range(HALVES)]
         for half, widths in enumerate([whole, in_two]):
-            r, one_minus_z = gates[half]
+            r, one_minus_z = stage_r_z(c, half, kept)
             stage_n(c, half, widths, r, one_minus_z, fresh)
         scatter(c, fresh, kept)

@@ -43,27 +43,26 @@ def tile_rnndecoder_kernel(tc, base, emb, ctx, h, w_ih, w_hh, b_ih, b_hh, offs, 
             (w_ih[256:512, :], ctx[0:256, :]),
             (w_ih[512:768, :], ctx[256:512, :]),
         ]
-        queues = [nc.sync, nc.scalar]
         slabs = [[], []]
         weight_tiles = []
         for d, (w_rows, x_rows) in enumerate(pairs):
             count = w_rows.shape[0] // P
             weights = held.tile([P, count, 3 * CHANNELS], BF16, name=f"weights{d}")
             first = held.tile([P, count, BANK], BF16, name=f"streams{d}_0")
-            queues[d % 2].dma_start(weights[:], w_rows.rearrange("(k p) m -> p k m", p=P))
-            queues[(d + 1) % 2].dma_start(first[:], x_rows.rearrange("(k p) n -> p k n", p=P)[:, :, 0:BANK])
+            nc.sync.dma_start(weights[:], w_rows.rearrange("(k p) m -> p k m", p=P))
+            nc.sync.dma_start(first[:], x_rows.rearrange("(k p) n -> p k n", p=P)[:, :, 0:BANK])
             weight_tiles.append(weights)
             slabs[0] += [(weights[:, k, :], first[:, k, :]) for k in range(count)]
 
         bias_rows = held.tile([P, P], F32, name="bias_rows")
         nc.gpsimd.memset(bias_rows[:], 0.0)
         nc.sync.dma_start(bias_rows[0 : 3 * BLOCKS, :], b_ih.rearrange("(g p) o -> g (p o)", p=P))
-        nc.scalar.dma_start(bias_rows[3 * BLOCKS : 6 * BLOCKS, :], b_hh.rearrange("(g p) o -> g (p o)", p=P))
+        nc.sync.dma_start(bias_rows[3 * BLOCKS : 6 * BLOCKS, :], b_hh.rearrange("(g p) o -> g (p o)", p=P))
 
         for d, (w_rows, x_rows) in enumerate(pairs):
             count = w_rows.shape[0] // P
             second = held.tile([P, count, BANK], BF16, name=f"streams{d}_1")
-            queues[(d + 1) % 2].dma_start(second[:], x_rows.rearrange("(k p) n -> p k n", p=P)[:, :, BANK:STREAMS])
+            nc.sync.dma_start(second[:], x_rows.rearrange("(k p) n -> p k n", p=P)[:, :, BANK:STREAMS])
             slabs[1] += [(weight_tiles[d][:, k, :], second[:, k, :]) for k in range(count)]
 
         offsets = held.tile([P, STREAMS // 16], U16, name="offsets")
@@ -71,9 +70,7 @@ def tile_rnndecoder_kernel(tc, base, emb, ctx, h, w_ih, w_hh, b_ih, b_hh, offs, 
 
         windows = [held.tile([P, SLOTS], F32, name=f"window{c}") for c in range(BLOCKS)]
         for c in range(BLOCKS):
-            for q, queue in enumerate(queues):
-                columns = slice(q * SLOTS // 2, (q + 1) * SLOTS // 2)
-                queue.dma_start(windows[c][:, columns], base[c * P : (c + 1) * P, columns])
+            nc.sync.dma_start(windows[c][:], base[c * P : (c + 1) * P, :])
 
         identity = held.tile([P, P], F32, name="identity")
         make_identity(nc, identity[:])

@@ -16,6 +16,7 @@ STREAMS = 1024
 SLOTS = 4096
 BANK = 512
 HALVES = STREAMS // BANK
+SLABS = 8
 PSUM_BANKS = 8
 R, Z, N = 0, 1, 2
 WARM_UP_MATMULS = 4
@@ -36,34 +37,25 @@ def tile_rnndecoder_kernel(tc, base, emb, ctx, h, w_ih, w_hh, b_ih, b_hh, offs, 
         for i in range(WARM_UP_MATMULS):
             nc.tensor.matmul(ps_start[:], zeros[:, 0:P], zeros[:], start=True, stop=True)
 
-        pairs = [
-            (w_hh[0:128, :], h[0:128, :]),
-            (w_hh[128:256, :], h[128:256, :]),
-            (w_ih[0:256, :], emb),
-            (w_ih[256:512, :], ctx[0:256, :]),
-            (w_ih[512:768, :], ctx[256:512, :]),
-        ]
+        weight_rows = [w[k * P : (k + 1) * P, :] for w in (w_hh, w_ih) for k in range(w.shape[0] // P)]
+        stream_rows = [x[k * P : (k + 1) * P, :] for x in (h, emb, ctx) for k in range(x.shape[0] // P)]
         slabs = [[], []]
-        weight_tiles = []
-        for d, (w_rows, x_rows) in enumerate(pairs):
-            count = w_rows.shape[0] // P
-            weights = held.tile([P, count, 3 * CHANNELS], BF16, name=f"weights{d}")
-            first = held.tile([P, count, BANK], BF16, name=f"streams{d}_0")
-            nc.sync.dma_start(weights[:], w_rows.rearrange("(k p) m -> p k m", p=P))
-            nc.sync.dma_start(first[:], x_rows.rearrange("(k p) n -> p k n", p=P)[:, :, 0:BANK])
-            weight_tiles.append(weights)
-            slabs[0] += [(weights[:, k, :], first[:, k, :]) for k in range(count)]
+        for s in range(SLABS):
+            weights = held.tile([P, 3 * CHANNELS], BF16, name=f"weights{s}")
+            first = held.tile([P, BANK], BF16, name=f"streams{s}_0")
+            nc.sync.dma_start(weights[:], weight_rows[s])
+            nc.sync.dma_start(first[:], stream_rows[s][:, 0:BANK])
+            slabs[0].append((weights[:], first[:]))
 
         bias_rows = held.tile([P, P], F32, name="bias_rows")
         nc.gpsimd.memset(bias_rows[:], 0.0)
         nc.sync.dma_start(bias_rows[0 : 3 * BLOCKS, :], b_ih.rearrange("(g p) o -> g (p o)", p=P))
         nc.sync.dma_start(bias_rows[3 * BLOCKS : 6 * BLOCKS, :], b_hh.rearrange("(g p) o -> g (p o)", p=P))
 
-        for d, (w_rows, x_rows) in enumerate(pairs):
-            count = w_rows.shape[0] // P
-            second = held.tile([P, count, BANK], BF16, name=f"streams{d}_1")
-            nc.sync.dma_start(second[:], x_rows.rearrange("(k p) n -> p k n", p=P)[:, :, BANK:STREAMS])
-            slabs[1] += [(weight_tiles[d][:, k, :], second[:, k, :]) for k in range(count)]
+        for s in range(SLABS):
+            second = held.tile([P, BANK], BF16, name=f"streams{s}_1")
+            nc.sync.dma_start(second[:], stream_rows[s][:, BANK:STREAMS])
+            slabs[1].append((slabs[0][s][0], second[:]))
 
         offsets = held.tile([P, STREAMS // 16], U16, name="offsets")
         nc.sync.dma_start(offsets[:], offs)

@@ -72,9 +72,9 @@ def tile_rnndecoder_kernel(tc, base, emb, ctx, h, w_ih, w_hh, b_ih, b_hh, offs, 
         bias_ih = bias_columns[:, 0 : 3 * BLOCKS]
         bias_hh = bias_columns[:, 3 * BLOCKS : 6 * BLOCKS]
         bias_sum = held.tile([P, 3 * BLOCKS], F32, name="bias_sum")
-        bias_neg = held.tile([P, 3 * BLOCKS], F32, name="bias_neg")
         nc.vector.tensor_tensor(bias_sum[:], bias_ih, bias_hh, ADD)
-        nc.vector.tensor_scalar_mul(bias_neg[:], bias_sum[:], -1.0)
+        bias_ih_neg = held.tile([P, 3 * BLOCKS], F32, name="bias_ih_neg")
+        nc.vector.tensor_scalar_mul(bias_ih_neg[:], bias_ih, -1.0)
 
         def multiply(products, half, columns=slice(0, BANK), by_slab=False):
             steps = [
@@ -90,82 +90,82 @@ def tile_rnndecoder_kernel(tc, base, emb, ctx, h, w_ih, w_hh, b_ih, b_hh, offs, 
                     bank[:], weights[:, gate_columns], activations[:, columns], start=is_first, stop=is_last
                 )
 
-        def gates_r_z(c, half, ps_r, ps_z, kept):
-            col_r, col_z = (slice(BLOCKS * g + c, BLOCKS * g + c + 1) for g in (R, Z))
-            r = work.tile([P, BANK], F32, name="r")
-            z = work.tile([P, BANK], F32, name="z")
-            one_minus_z = work.tile([P, BANK], F32, name="one_minus_z")
-            nc.scalar.activation(r[:], ps_r[:], SIGMOID, bias=bias_sum[:, col_r])
-            nc.scalar.activation(z[:], ps_z[:], SIGMOID, bias=bias_sum[:, col_z])
-            nc.scalar.activation(one_minus_z[:], ps_z[:], SIGMOID, bias=bias_neg[:, col_z], scale=-1.0)
-            nc.gpsimd.tensor_tensor(kept[:, half * BANK : (half + 1) * BANK], z[:], slabs[half][c][1], MULT)
-            return r, one_minus_z
+        def gate_columns(gate, c):
+            return slice(gate * CHANNELS + c * P, gate * CHANNELS + (c + 1) * P)
 
-        def reset_v_n(c, ps_vn, r):
+        def bias_column(biases, gate, c):
+            return biases[:, BLOCKS * gate + c : BLOCKS * gate + c + 1]
+
+        def new_bank(width=BANK):
+            return psum.tile([P, width], F32, name="product")
+
+        def product(gate, c, half, begin, end, columns=slice(0, BANK)):
+            bank = new_bank(columns.stop - columns.start)
+            multiply([(bank, gate_columns(gate, c), begin, end)], half, columns)
+            return bank
+
+        def sigmoid(ps, gate, c):
+            width = ps.shape[1]
+            s = work.tile([P, width], F32, name=f"gate{gate}_{width}", bufs=3)
+            nc.scalar.activation(s[:], ps[:], SIGMOID, bias=bias_column(bias_sum, gate, c))
+            return s
+
+        def reset(c, ps_vn, r):
             r_vn = work.tile([P, BANK], F32, name="r_vn")
-            nc.vector.scalar_tensor_tensor(
-                r_vn[:], ps_vn[:], bias_hh[:, BLOCKS * N + c : BLOCKS * N + c + 1], r[:], ADD, MULT
-            )
+            nc.vector.scalar_tensor_tensor(r_vn[:], ps_vn[:], bias_column(bias_hh, N, c), r[:], ADD, MULT)
             return r_vn
 
-        def gate_n(c, half, columns, ps_un, r_vn, one_minus_z, fresh):
-            width = columns.stop - columns.start
-            pre_n = work.tile([P, width], F32, name="pre_n")
-            n = work.tile([P, width], F32, name="n")
-            nc.vector.tensor_tensor(pre_n[:], r_vn[:, columns], ps_un[:], ADD)
-            nc.scalar.activation(n[:], pre_n[:], TANH, bias=bias_ih[:, BLOCKS * N + c : BLOCKS * N + c + 1])
-            nc.vector.tensor_tensor(
-                fresh[:, half * BANK + columns.start : half * BANK + columns.stop], one_minus_z[:, columns], n[:], MULT
-            )
+        def candidate(c, r_vn, ps_un):
+            pre_n = work.tile([P, BANK], F32, name="pre_n")
+            minus_n = work.tile([P, BANK], F32, name="minus_n")
+            nc.vector.tensor_tensor(pre_n[:], r_vn[:], ps_un[:], ADD)
+            nc.scalar.activation(minus_n[:], pre_n[:], TANH, bias=bias_column(bias_ih_neg, N, c), scale=-1.0)
+            return minus_n
+
+        def mix(c, half, columns, z, minus_n, fresh, kept, kept_engine):
+            placed = slice(half * BANK + columns.start, half * BANK + columns.stop)
+            kept_engine.tensor_tensor(kept[:, placed], z[:], slabs[half][c][1][:, columns], MULT)
+            nc.vector.scalar_tensor_tensor(fresh[:, placed], z[:], -1.0, minus_n[:, columns], ADD, MULT)
+
+        def z_last(c, half, widths, minus_n, fresh, kept):
+            left = 0
+            for width in widths:
+                columns = slice(left, left + width)
+                z = sigmoid(product(Z, c, half, 0, 8, columns), Z, c)
+                mix(c, half, columns, z, minus_n, fresh, kept, nc.vector)
+                left += width
 
         def scatter(c, fresh, kept):
             nc.vector.tensor_tensor(windows[c][:].indirect(offsets[:]), fresh[:], kept[:], ADD)
             nc.sync.dma_start(out[c * P : (c + 1) * P, :], windows[c][:])
 
-        def gate_columns_of(c):
-            return (slice(g * CHANNELS + c * P, g * CHANNELS + (c + 1) * P) for g in (R, Z, N))
-
-        def new_bank(width=BANK):
-            return psum.tile([P, width], F32, name="product")
-
-        def stage_r_z(c, half, kept):
-            w_r, w_z, w_n = gate_columns_of(c)
-            ps_r, ps_z = new_bank(), new_bank()
-            multiply([(ps_r, w_r, 0, 8), (ps_z, w_z, 0, 8)], half)
-            return gates_r_z(c, half, ps_r, ps_z, kept)
-
-        def stage_n(c, half, widths, r, one_minus_z, fresh):
-            w_r, w_z, w_n = gate_columns_of(c)
-            ps_vn = new_bank()
-            multiply([(ps_vn, w_n, 0, 2)], half)
-            r_vn = reset_v_n(c, ps_vn, r)
-            left = 0
-            for width in widths:
-                columns = slice(left, left + width)
-                ps_un = new_bank(width)
-                multiply([(ps_un, w_n, 2, 8)], half, columns)
-                gate_n(c, half, columns, ps_un, r_vn, one_minus_z, fresh)
-                left += width
-
-        whole, in_two = [BANK], [BANK // 2, BANK // 2]
+        whole, halving = slice(0, BANK), [BANK // 2, BANK // 4, BANK // 4]
 
         c = 0
-        w_r, w_z, w_n = gate_columns_of(c)
         fresh = work.tile([P, STREAMS], F32, name="fresh")
         kept = work.tile([P, STREAMS], F32, name="kept")
         ps_vn, ps_r, ps_z, ps_un = new_bank(), new_bank(), new_bank(), new_bank()
+        w_r, w_z, w_n = (gate_columns(g, c) for g in (R, Z, N))
         multiply([(ps_vn, w_n, 0, 2), (ps_r, w_r, 0, 8), (ps_z, w_z, 0, 8), (ps_un, w_n, 2, 8)], 0, by_slab=True)
-        r, one_minus_z = gates_r_z(c, 0, ps_r, ps_z, kept)
-        r_vn = reset_v_n(c, ps_vn, r)
-        gate_n(c, 0, slice(0, BANK), ps_un, r_vn, one_minus_z, fresh)
-        r, one_minus_z = stage_r_z(c, 1, kept)
-        stage_n(c, 1, in_two, r, one_minus_z, fresh)
+        r, z = sigmoid(ps_r, R, c), sigmoid(ps_z, Z, c)
+        minus_n = candidate(c, reset(c, ps_vn, r), ps_un)
+        mix(c, 0, whole, z, minus_n, fresh, kept, nc.gpsimd)
+        r = sigmoid(product(R, c, 1, 0, 8), R, c)
+        r_vn = reset(c, product(N, c, 1, 0, 2), r)
+        minus_n = candidate(c, r_vn, product(N, c, 1, 2, 8))
+        z_last(c, 1, halving, minus_n, fresh, kept)
         scatter(c, fresh, kept)
 
         c = 1
         fresh = work.tile([P, STREAMS], F32, name="fresh")
         kept = work.tile([P, STREAMS], F32, name="kept")
-        for half, widths in enumerate([whole, in_two]):
-            r, one_minus_z = stage_r_z(c, half, kept)
-            stage_n(c, half, widths, r, one_minus_z, fresh)
+        r_0 = sigmoid(product(R, c, 0, 0, 8), R, c)
+        z_0 = sigmoid(product(Z, c, 0, 0, 8), Z, c)
+        r_1 = sigmoid(product(R, c, 1, 0, 8), R, c)
+        r_vn_0 = reset(c, product(N, c, 0, 0, 2), r_0)
+        r_vn_1 = reset(c, product(N, c, 1, 0, 2), r_1)
+        minus_n_0 = candidate(c, r_vn_0, product(N, c, 0, 2, 8))
+        minus_n = candidate(c, r_vn_1, product(N, c, 1, 2, 8))
+        mix(c, 0, whole, z_0, minus_n_0, fresh, kept, nc.gpsimd)
+        z_last(c, 1, halving, minus_n, fresh, kept)
         scatter(c, fresh, kept)

@@ -17,6 +17,7 @@ SLOTS = 4096
 BANK = 512
 HALVES = STREAMS // BANK
 SLABS = 8
+CTX_SLABS = range(4, SLABS)
 PSUM_BANKS = 8
 R, Z, N = 0, 1, 2
 WARM_UP_MATMULS = 4
@@ -37,8 +38,18 @@ def tile_rnndecoder_kernel(tc, base, emb, ctx, h, w_ih, w_hh, b_ih, b_hh, offs, 
         for i in range(WARM_UP_MATMULS):
             nc.tensor.matmul(ps_start[:], zeros[:, 0:P], zeros[:], start=True, stop=True)
 
+        table_loaded = held.tile([P, 1], F32, name="table_loaded")
+        nc.scalar.activation(table_loaded[:], zeros[:, 0:1], SIGMOID)
+
         weight_rows = [w[k * P : (k + 1) * P, :] for w in (w_hh, w_ih) for k in range(w.shape[0] // P)]
         stream_rows = [x[k * P : (k + 1) * P, :] for x in (h, emb, ctx) for k in range(x.shape[0] // P)]
+        bias_rows = held.tile([P, P], F32, name="bias_rows")
+        nc.gpsimd.memset(bias_rows[:], 0.0)
+        nc.gpsimd.dma_start(bias_rows[0 : 3 * BLOCKS, :], b_ih.rearrange("(g p) o -> g (p o)", p=P))
+        nc.gpsimd.dma_start(bias_rows[3 * BLOCKS : 6 * BLOCKS, :], b_hh.rearrange("(g p) o -> g (p o)", p=P))
+        identity = held.tile([P, P], F32, name="identity")
+        make_identity(nc, identity[:])
+
         slabs = [[], []]
         for s in range(SLABS):
             weights = held.tile([P, 3 * CHANNELS], BF16, name=f"weights{s}")
@@ -47,15 +58,11 @@ def tile_rnndecoder_kernel(tc, base, emb, ctx, h, w_ih, w_hh, b_ih, b_hh, offs, 
             nc.sync.dma_start(first[:], stream_rows[s][:, 0:BANK])
             slabs[0].append((weights[:], first[:]))
 
-        bias_rows = held.tile([P, P], F32, name="bias_rows")
-        nc.gpsimd.memset(bias_rows[:], 0.0)
-        nc.sync.dma_start(bias_rows[0 : 3 * BLOCKS, :], b_ih.rearrange("(g p) o -> g (p o)", p=P))
-        nc.sync.dma_start(bias_rows[3 * BLOCKS : 6 * BLOCKS, :], b_hh.rearrange("(g p) o -> g (p o)", p=P))
-
-        for s in range(SLABS):
-            second = held.tile([P, BANK], BF16, name=f"streams{s}_1")
-            nc.sync.dma_start(second[:], stream_rows[s][:, BANK:STREAMS])
-            slabs[1].append((slabs[0][s][0], second[:]))
+        for name, x in (("h", h), ("emb", emb), ("ctx", ctx)):
+            second = held.tile([P, x.shape[0] // P, BANK], BF16, name=f"{name}_1")
+            nc.sync.dma_start(second[:], x.rearrange("(k p) n -> p k n", p=P)[:, :, BANK:STREAMS])
+            for k in range(x.shape[0] // P):
+                slabs[1].append((slabs[0][len(slabs[1])][0], second[:, k, :]))
 
         offsets = held.tile([P, STREAMS // 16], U16, name="offsets")
         nc.sync.dma_start(offsets[:], offs)
@@ -64,31 +71,18 @@ def tile_rnndecoder_kernel(tc, base, emb, ctx, h, w_ih, w_hh, b_ih, b_hh, offs, 
         for c in range(BLOCKS):
             nc.sync.dma_start(windows[c][:], base[c * P : (c + 1) * P, :])
 
-        identity = held.tile([P, P], F32, name="identity")
-        make_identity(nc, identity[:])
-        nc.tensor.transpose(ps_start[:, 0:P], bias_rows[:], identity[:])
-        bias_columns = held.tile([P, 6 * BLOCKS], F32, name="bias_columns")
-        nc.vector.tensor_copy(bias_columns[:], ps_start[:, 0 : 6 * BLOCKS])
-        bias_ih = bias_columns[:, 0 : 3 * BLOCKS]
-        bias_hh = bias_columns[:, 3 * BLOCKS : 6 * BLOCKS]
-        bias_sum = held.tile([P, 3 * BLOCKS], F32, name="bias_sum")
-        nc.vector.tensor_tensor(bias_sum[:], bias_ih, bias_hh, ADD)
-        bias_ih_neg = held.tile([P, 3 * BLOCKS], F32, name="bias_ih_neg")
-        nc.vector.tensor_scalar_mul(bias_ih_neg[:], bias_ih, -1.0)
-
-        def multiply(products, half, columns=slice(0, BANK), by_slab=False):
-            steps = [
-                (s, bank, gate_columns, s == begin, s == end - 1)
-                for bank, gate_columns, begin, end in products
-                for s in range(begin, end)
-            ]
-            if by_slab:
-                steps = sorted(steps, key=lambda step: step[0])
-            for s, bank, gate_columns, is_first, is_last in steps:
-                weights, activations = slabs[half][s]
-                nc.tensor.matmul(
-                    bank[:], weights[:, gate_columns], activations[:, columns], start=is_first, stop=is_last
-                )
+        def multiply(products, half, columns=slice(0, BANK), only=range(SLABS)):
+            for bank, gate_columns, begin, end in products:
+                for s in range(begin, end):
+                    if s in only:
+                        weights, activations = slabs[half][s]
+                        nc.tensor.matmul(
+                            bank[:],
+                            weights[:, gate_columns],
+                            activations[:, columns],
+                            start=s == begin,
+                            stop=s == end - 1,
+                        )
 
         def gate_columns(gate, c):
             return slice(gate * CHANNELS + c * P, gate * CHANNELS + (c + 1) * P)
@@ -146,7 +140,22 @@ def tile_rnndecoder_kernel(tc, base, emb, ctx, h, w_ih, w_hh, b_ih, b_hh, offs, 
         kept = work.tile([P, STREAMS], F32, name="kept")
         ps_vn, ps_r, ps_z, ps_un = new_bank(), new_bank(), new_bank(), new_bank()
         w_r, w_z, w_n = (gate_columns(g, c) for g in (R, Z, N))
-        multiply([(ps_vn, w_n, 0, 2), (ps_r, w_r, 0, 8), (ps_z, w_z, 0, 8), (ps_un, w_n, 2, 8)], 0, by_slab=True)
+        first_unit = [(ps_vn, w_n, 0, 2), (ps_r, w_r, 0, 8), (ps_z, w_z, 0, 8), (ps_un, w_n, 2, 8)]
+        for s in range(CTX_SLABS.start):
+            multiply(first_unit, 0, only=[s])
+
+        nc.tensor.transpose(ps_start[:, 0:P], bias_rows[:], identity[:])
+        bias_columns = held.tile([P, 6 * BLOCKS], F32, name="bias_columns")
+        nc.vector.tensor_copy(bias_columns[:], ps_start[:, 0 : 6 * BLOCKS])
+        bias_ih = bias_columns[:, 0 : 3 * BLOCKS]
+        bias_hh = bias_columns[:, 3 * BLOCKS : 6 * BLOCKS]
+        bias_sum = held.tile([P, 3 * BLOCKS], F32, name="bias_sum")
+        nc.vector.tensor_tensor(bias_sum[:], bias_ih, bias_hh, ADD)
+        bias_ih_neg = held.tile([P, 3 * BLOCKS], F32, name="bias_ih_neg")
+        nc.vector.tensor_scalar_mul(bias_ih_neg[:], bias_ih, -1.0)
+
+        for s in CTX_SLABS:
+            multiply(first_unit, 0, only=[s])
         r, z = sigmoid(ps_r, R, c), sigmoid(ps_z, Z, c)
         minus_n = candidate(c, reset(c, ps_vn, r), ps_un)
         mix(c, 0, whole, z, minus_n, fresh, kept, nc.gpsimd)

@@ -20,7 +20,7 @@ SLABS = 8
 CTX_SLABS = range(4, SLABS)
 PSUM_BANKS = 8
 R, Z, N = 0, 1, 2
-WARM_UP_MATMULS = 4
+WARM_UP_MATMULS = 13
 
 FLOPS = 2 * STREAMS * 3 * CHANNELS * (768 + CHANNELS)
 
@@ -32,11 +32,11 @@ def tile_rnndecoder_kernel(tc, base, emb, ctx, h, w_ih, w_hh, b_ih, b_hh, offs, 
         tc.tile_pool(name="work", bufs=2) as work,
         tc.psum_pool(name="psum", bufs=PSUM_BANKS) as psum,
     ):
-        zeros = held.tile([P, BANK], BF16, name="zeros")
+        zeros = held.tile([P, P], BF16, name="zeros")
         nc.vector.memset(zeros[:], 0.0)
         ps_start = psum.tile([P, BANK], F32, name="ps_start", tag="product")
         for i in range(WARM_UP_MATMULS):
-            nc.tensor.matmul(ps_start[:], zeros[:, 0:P], zeros[:], start=True, stop=True)
+            nc.tensor.matmul(ps_start[:, 0:P], zeros[:], zeros[:], start=True, stop=True)
 
         table_loaded = held.tile([P, 1], F32, name="table_loaded")
         nc.scalar.activation(table_loaded[:], zeros[:, 0:1], SIGMOID)
@@ -54,8 +54,11 @@ def tile_rnndecoder_kernel(tc, base, emb, ctx, h, w_ih, w_hh, b_ih, b_hh, offs, 
         for s in range(SLABS):
             weights = held.tile([P, 3 * CHANNELS], BF16, name=f"weights{s}")
             first = held.tile([P, BANK], BF16, name=f"streams{s}_0")
-            nc.sync.dma_start(weights[:], weight_rows[s])
+            pieces = [slice(N * CHANNELS, 3 * CHANNELS), slice(0, N * CHANNELS)] if s == 0 else [slice(0, 3 * CHANNELS)]
+            nc.sync.dma_start(weights[:, pieces[0]], weight_rows[s][:, pieces[0]])
             nc.sync.dma_start(first[:], stream_rows[s][:, 0:BANK])
+            for piece in pieces[1:]:
+                nc.sync.dma_start(weights[:, piece], weight_rows[s][:, piece])
             slabs[0].append((weights[:], first[:]))
 
         for name, x in (("h", h), ("emb", emb), ("ctx", ctx)):

@@ -60,12 +60,15 @@ def tile_rnndecoder_kernel(tc, base, emb, ctx, h, w_ih, w_hh, b_ih, b_hh, offs, 
             for piece in pieces[1:]:
                 nc.sync.dma_start(weights[:, piece], weight_rows[s][:, piece])
             slabs[0].append((weights[:], first[:]))
+            if s not in CTX_SLABS:
+                second = held.tile([P, BANK], BF16, name=f"streams{s}_1")
+                nc.sync.dma_start(second[:], stream_rows[s][:, BANK:STREAMS])
+                slabs[1].append((weights[:], second[:]))
 
-        for name, x in (("h", h), ("emb", emb), ("ctx", ctx)):
-            second = held.tile([P, x.shape[0] // P, BANK], BF16, name=f"{name}_1")
-            nc.sync.dma_start(second[:], x.rearrange("(k p) n -> p k n", p=P)[:, :, BANK:STREAMS])
-            for k in range(x.shape[0] // P):
-                slabs[1].append((slabs[0][len(slabs[1])][0], second[:, k, :]))
+        second = held.tile([P, len(CTX_SLABS), BANK], BF16, name="ctx_1")
+        nc.sync.dma_start(second[:], ctx.rearrange("(k p) n -> p k n", p=P)[:, :, BANK:STREAMS])
+        for k, s in enumerate(CTX_SLABS):
+            slabs[1].append((slabs[0][s][0], second[:, k, :]))
 
         offsets = held.tile([P, STREAMS // 16], U16, name="offsets")
         nc.sync.dma_start(offsets[:], offs)
@@ -144,8 +147,11 @@ def tile_rnndecoder_kernel(tc, base, emb, ctx, h, w_ih, w_hh, b_ih, b_hh, offs, 
         ps_vn, ps_r, ps_z, ps_un = new_bank(), new_bank(), new_bank(), new_bank()
         w_r, w_z, w_n = (gate_columns(g, c) for g in (R, Z, N))
         first_unit = [(ps_vn, w_n, 0, 2), (ps_r, w_r, 0, 8), (ps_z, w_z, 0, 8), (ps_un, w_n, 2, 8)]
+        ps_vn_1, ps_r_1, ps_un_1 = new_bank(), new_bank(), new_bank()
+        second_unit = [(ps_vn_1, w_n, 0, 2), (ps_r_1, w_r, 0, 8), (ps_un_1, w_n, 2, 8)]
         for s in range(CTX_SLABS.start):
             multiply(first_unit, 0, only=[s])
+            multiply(second_unit, 1, only=[s])
 
         nc.tensor.transpose(ps_start[:, 0:P], bias_rows[:], identity[:])
         bias_columns = held.tile([P, 6 * BLOCKS], F32, name="bias_columns")
@@ -162,9 +168,9 @@ def tile_rnndecoder_kernel(tc, base, emb, ctx, h, w_ih, w_hh, b_ih, b_hh, offs, 
         r, z = sigmoid(ps_r, R, c), sigmoid(ps_z, Z, c)
         minus_n = candidate(c, reset(c, ps_vn, r), ps_un)
         mix(c, 0, whole, z, minus_n, fresh, kept, nc.gpsimd)
-        r = sigmoid(product(R, c, 1, 0, 8), R, c)
-        r_vn = reset(c, product(N, c, 1, 0, 2), r)
-        minus_n = candidate(c, r_vn, product(N, c, 1, 2, 8))
+        multiply(second_unit, 1, only=CTX_SLABS)
+        r = sigmoid(ps_r_1, R, c)
+        minus_n = candidate(c, reset(c, ps_vn_1, r), ps_un_1)
         z_last(c, 1, halving, minus_n, fresh, kept)
         scatter(c, fresh, kept)
 

@@ -17,7 +17,7 @@ SLOTS = 4096
 BANK = 512
 HALVES = STREAMS // BANK
 SLABS = 8
-CTX_SLABS = range(4, SLABS)
+H_SLABS, EMB_SLABS, CTX_SLABS = range(0, 2), range(2, 4), range(4, SLABS)
 PSUM_BANKS = 8
 R, Z, N = 0, 1, 2
 WARM_UP_MATMULS = 13
@@ -41,8 +41,6 @@ def tile_rnndecoder_kernel(tc, base, emb, ctx, h, w_ih, w_hh, b_ih, b_hh, offs, 
         table_loaded = held.tile([P, 1], F32, name="table_loaded")
         nc.scalar.activation(table_loaded[:], zeros[:, 0:1], SIGMOID)
 
-        weight_rows = [w[k * P : (k + 1) * P, :] for w in (w_hh, w_ih) for k in range(w.shape[0] // P)]
-        stream_rows = [x[k * P : (k + 1) * P, :] for x in (h, emb, ctx) for k in range(x.shape[0] // P)]
         bias_rows = held.tile([P, P], F32, name="bias_rows")
         nc.gpsimd.memset(bias_rows[:], 0.0)
         nc.gpsimd.dma_start(bias_rows[0 : 3 * BLOCKS, :], b_ih.rearrange("(g p) o -> g (p o)", p=P))
@@ -51,24 +49,37 @@ def tile_rnndecoder_kernel(tc, base, emb, ctx, h, w_ih, w_hh, b_ih, b_hh, offs, 
         make_identity(nc, identity[:])
 
         slabs = [[], []]
-        for s in range(SLABS):
+        rows = [(w_hh, h, k) for k in range(len(H_SLABS))] + [(w_ih, emb, k) for k in range(len(EMB_SLABS))]
+        for s, (w, x, k) in enumerate(rows):
             weights = held.tile([P, 3 * CHANNELS], BF16, name=f"weights{s}")
-            first = held.tile([P, BANK], BF16, name=f"streams{s}_0")
-            pieces = [slice(N * CHANNELS, 3 * CHANNELS), slice(0, N * CHANNELS)] if s == 0 else [slice(0, 3 * CHANNELS)]
-            nc.sync.dma_start(weights[:, pieces[0]], weight_rows[s][:, pieces[0]])
-            nc.sync.dma_start(first[:], stream_rows[s][:, 0:BANK])
-            for piece in pieces[1:]:
-                nc.sync.dma_start(weights[:, piece], weight_rows[s][:, piece])
-            slabs[0].append((weights[:], first[:]))
-            if s not in CTX_SLABS:
-                second = held.tile([P, BANK], BF16, name=f"streams{s}_1")
-                nc.sync.dma_start(second[:], stream_rows[s][:, BANK:STREAMS])
-                slabs[1].append((weights[:], second[:]))
+            streams = held.tile([P, STREAMS], BF16, name=f"streams{s}")
+            block = slice(k * P, (k + 1) * P)
+            if s == 0:
+                for tile, source, columns in (
+                    (weights, w, slice(N * CHANNELS, 3 * CHANNELS)),
+                    (streams, x, slice(0, BANK)),
+                    (weights, w, slice(0, N * CHANNELS)),
+                    (streams, x, slice(BANK, STREAMS)),
+                ):
+                    nc.sync.dma_start(tile[:, columns], source[block, columns])
+            else:
+                nc.sync.dma_start(weights[:], w[block, :])
+                nc.sync.dma_start(streams[:], x[block, :])
+            for half in range(HALVES):
+                slabs[half].append((weights[:], streams[:, half * BANK : (half + 1) * BANK]))
 
+        ctx_rows = ctx.rearrange("(p k) n -> p k n", p=P)
+        ctx_weight_rows = w_ih[2 * P :, :].rearrange("(p k) m -> p k m", p=P)
         second = held.tile([P, len(CTX_SLABS), BANK], BF16, name="ctx_1")
-        nc.sync.dma_start(second[:], ctx.rearrange("(k p) n -> p k n", p=P)[:, :, BANK:STREAMS])
-        for k, s in enumerate(CTX_SLABS):
-            slabs[1].append((slabs[0][s][0], second[:, k, :]))
+        for pair in range(0, len(CTX_SLABS), 2):
+            weights = held.tile([P, 2, 3 * CHANNELS], BF16, name=f"ctx_weights{pair}")
+            first = held.tile([P, 2, BANK], BF16, name=f"ctx_0_{pair}")
+            nc.sync.dma_start(weights[:], ctx_weight_rows[:, pair : pair + 2, :])
+            nc.sync.dma_start(first[:], ctx_rows[:, pair : pair + 2, 0:BANK])
+            for k in range(2):
+                slabs[0].append((weights[:, k, :], first[:, k, :]))
+                slabs[1].append((weights[:, k, :], second[:, pair + k, :]))
+        nc.sync.dma_start(second[:], ctx_rows[:, :, BANK:STREAMS])
 
         offsets = held.tile([P, STREAMS // 16], U16, name="offsets")
         nc.sync.dma_start(offsets[:], offs)

@@ -133,9 +133,9 @@ def tile_rnndecoder_kernel(tc, base, emb, ctx, h, w_ih, w_hh, b_ih, b_hh, offs, 
             nc.scalar.activation(minus_n[:], pre_n[:], TANH, bias=bias_column(bias_ih_neg, N, c), scale=-1.0)
             return minus_n
 
-        def mix(c, half, columns, z, minus_n, fresh, kept, kept_engine):
+        def mix(c, half, columns, z, minus_n, fresh, kept):
             placed = slice(half * BANK + columns.start, half * BANK + columns.stop)
-            kept_engine.tensor_tensor(kept[:, placed], z[:], slabs[half][c][1][:, columns], MULT)
+            nc.vector.tensor_tensor(kept[:, placed], z[:], slabs[half][c][1][:, columns], MULT)
             nc.vector.scalar_tensor_tensor(fresh[:, placed], z[:], -1.0, minus_n[:, columns], ADD, MULT)
 
         def z_last(c, half, widths, minus_n, fresh, kept):
@@ -143,7 +143,7 @@ def tile_rnndecoder_kernel(tc, base, emb, ctx, h, w_ih, w_hh, b_ih, b_hh, offs, 
             for width in widths:
                 columns = slice(left, left + width)
                 z = sigmoid(product(Z, c, half, 0, 8, columns), Z, c)
-                mix(c, half, columns, z, minus_n, fresh, kept, nc.vector)
+                mix(c, half, columns, z, minus_n, fresh, kept)
                 left += width
 
         def scatter(c, fresh, kept):
@@ -178,7 +178,7 @@ def tile_rnndecoder_kernel(tc, base, emb, ctx, h, w_ih, w_hh, b_ih, b_hh, offs, 
             multiply(first_unit, 0, only=[s])
         r, z = sigmoid(ps_r, R, c), sigmoid(ps_z, Z, c)
         minus_n = candidate(c, reset(c, ps_vn, r), ps_un)
-        mix(c, 0, whole, z, minus_n, fresh, kept, nc.gpsimd)
+        mix(c, 0, whole, z, minus_n, fresh, kept)
         multiply(second_unit, 1, only=CTX_SLABS)
         r = sigmoid(ps_r_1, R, c)
         minus_n = candidate(c, reset(c, ps_vn_1, r), ps_un_1)
@@ -195,6 +195,6 @@ def tile_rnndecoder_kernel(tc, base, emb, ctx, h, w_ih, w_hh, b_ih, b_hh, offs, 
         r_vn_1 = reset(c, product(N, c, 1, 0, 2), r_1)
         minus_n_0 = candidate(c, r_vn_0, product(N, c, 0, 2, 8))
         minus_n = candidate(c, r_vn_1, product(N, c, 1, 2, 8))
-        mix(c, 0, whole, z_0, minus_n_0, fresh, kept, nc.gpsimd)
+        mix(c, 0, whole, z_0, minus_n_0, fresh, kept)
         z_last(c, 1, halving, minus_n, fresh, kept)
         scatter(c, fresh, kept)

import concourse.mybir as mybir
from concourse.masks import make_identity

F32 = mybir.dt.float32
BF16 = mybir.dt.bfloat16
U16 = mybir.dt.uint16
ADD = mybir.AluOpType.add
MULT = mybir.AluOpType.mult
SIGMOID = mybir.ActivationFunctionType.Sigmoid
TANH = mybir.ActivationFunctionType.Tanh

P = 128
CHANNELS = 256
BLOCKS = CHANNELS // P
STREAMS = 1024
SLOTS = 4096
BANK = 512
HALVES = STREAMS // BANK
SLABS = 8
H_SLABS, EMB_SLABS, CTX_SLABS = range(0, 2), range(2, 4), range(4, SLABS)
PSUM_BANKS = 8
R, Z, N = 0, 1, 2
WARM_UP_MATMULS = 13

FLOPS = 2 * STREAMS * 3 * CHANNELS * (768 + CHANNELS)


def tile_rnndecoder_kernel(tc, base, emb, ctx, h, w_ih, w_hh, b_ih, b_hh, offs, out):
    nc = tc.nc
    with (
        tc.tile_pool(name="held", bufs=1) as held,
        tc.tile_pool(name="work", bufs=2) as work,
        tc.psum_pool(name="psum", bufs=PSUM_BANKS) as psum,
    ):
        zeros = held.tile([P, P], BF16, name="zeros")
        nc.vector.memset(zeros[:], 0.0)
        ps_start = psum.tile([P, BANK], F32, name="ps_start", tag="product")
        for i in range(WARM_UP_MATMULS):
            nc.tensor.matmul(ps_start[:, 0:P], zeros[:], zeros[:], start=True, stop=True)

        table_loaded = held.tile([P, 1], F32, name="table_loaded")
        nc.scalar.activation(table_loaded[:], zeros[:, 0:1], SIGMOID)

        bias_rows = held.tile([P, P], F32, name="bias_rows")
        nc.gpsimd.memset(bias_rows[:], 0.0)
        nc.gpsimd.dma_start(bias_rows[0 : 3 * BLOCKS, :], b_ih.rearrange("(g p) o -> g (p o)", p=P))
        nc.gpsimd.dma_start(bias_rows[3 * BLOCKS : 6 * BLOCKS, :], b_hh.rearrange("(g p) o -> g (p o)", p=P))
        identity = held.tile([P, P], F32, name="identity")
        make_identity(nc, identity[:])

        slabs = [[], []]
        rows = [(w_hh, h, k) for k in range(len(H_SLABS))] + [(w_ih, emb, k) for k in range(len(EMB_SLABS))]
        for s, (w, x, k) in enumerate(rows):
            weights = held.tile([P, 3 * CHANNELS], BF16, name=f"weights{s}")
            streams = held.tile([P, STREAMS], BF16, name=f"streams{s}")
            block = slice(k * P, (k + 1) * P)
            if s == 0:
                for tile, source, columns in (
                    (weights, w, slice(N * CHANNELS, 3 * CHANNELS)),
                    (streams, x, slice(0, BANK)),
                    (weights, w, slice(0, N * CHANNELS)),
                    (streams, x, slice(BANK, STREAMS)),
                ):
                    nc.sync.dma_start(tile[:, columns], source[block, columns])
            else:
                nc.sync.dma_start(weights[:], w[block, :])
                nc.sync.dma_start(streams[:], x[block, :])
            for half in range(HALVES):
                slabs[half].append((weights[:], streams[:, half * BANK : (half + 1) * BANK]))

        ctx_rows = ctx.rearrange("(p k) n -> p k n", p=P)
        ctx_weight_rows = w_ih[2 * P :, :].rearrange("(p k) m -> p k m", p=P)
        second = held.tile([P, len(CTX_SLABS), BANK], BF16, name="ctx_1")
        for pair in range(0, len(CTX_SLABS), 2):
            weights = held.tile([P, 2, 3 * CHANNELS], BF16, name=f"ctx_weights{pair}")
            first = held.tile([P, 2, BANK], BF16, name=f"ctx_0_{pair}")
            nc.sync.dma_start(weights[:], ctx_weight_rows[:, pair : pair + 2, :])
            nc.sync.dma_start(first[:], ctx_rows[:, pair : pair + 2, 0:BANK])
            for k in range(2):
                slabs[0].append((weights[:, k, :], first[:, k, :]))
                slabs[1].append((weights[:, k, :], second[:, pair + k, :]))
        nc.sync.dma_start(second[:], ctx_rows[:, :, BANK:STREAMS])

        offsets = held.tile([P, STREAMS // 16], U16, name="offsets")
        nc.sync.dma_start(offsets[:], offs)

        windows = [held.tile([P, SLOTS], F32, name=f"window{c}") for c in range(BLOCKS)]
        for c in range(BLOCKS):
            nc.sync.dma_start(windows[c][:], base[c * P : (c + 1) * P, :])

        def multiply(products, half, columns=slice(0, BANK), only=range(SLABS)):
            for bank, gate_columns, begin, end in products:
                for s in range(begin, end):
                    if s in only:
                        weights, activations = slabs[half][s]
                        nc.tensor.matmul(
                            bank[:],
                            weights[:, gate_columns],
                            activations[:, columns],
                            start=s == begin,
                            stop=s == end - 1,
                        )

        def gate_columns(gate, c):
            return slice(gate * CHANNELS + c * P, gate * CHANNELS + (c + 1) * P)

        def bias_column(biases, gate, c):
            return biases[:, BLOCKS * gate + c : BLOCKS * gate + c + 1]

        def new_bank(width=BANK):
            return psum.tile([P, width], F32, name="product")

        def product(gate, c, half, begin, end, columns=slice(0, BANK)):
            bank = new_bank(columns.stop - columns.start)
            multiply([(bank, gate_columns(gate, c), begin, end)], half, columns)
            return bank

        def sigmoid(ps, gate, c):
            width = ps.shape[1]
            s = work.tile([P, width], F32, name=f"gate{gate}_{width}", bufs=3)
            nc.scalar.activation(s[:], ps[:], SIGMOID, bias=bias_column(bias_sum, gate, c))
            return s

        def reset(c, ps_vn, r):
            r_vn = work.tile([P, BANK], F32, name="r_vn")
            nc.vector.scalar_tensor_tensor(r_vn[:], ps_vn[:], bias_column(bias_hh, N, c), r[:], ADD, MULT)
            return r_vn

        def candidate(c, r_vn, ps_un):
            pre_n = work.tile([P, BANK], F32, name="pre_n")
            minus_n = work.tile([P, BANK], F32, name="minus_n")
            nc.vector.tensor_tensor(pre_n[:], r_vn[:], ps_un[:], ADD)
            nc.scalar.activation(minus_n[:], pre_n[:], TANH, bias=bias_column(bias_ih_neg, N, c), scale=-1.0)
            return minus_n

        def mix(c, half, columns, z, minus_n, fresh, kept):
            placed = slice(half * BANK + columns.start, half * BANK + columns.stop)
            nc.vector.tensor_tensor(kept[:, placed], z[:], slabs[half][c][1][:, columns], MULT)
            nc.vector.scalar_tensor_tensor(fresh[:, placed], z[:], -1.0, minus_n[:, columns], ADD, MULT)

        def z_last(c, half, widths, minus_n, fresh, kept):
            left = 0
            for width in widths:
                columns = slice(left, left + width)
                z = sigmoid(product(Z, c, half, 0, 8, columns), Z, c)
                mix(c, half, columns, z, minus_n, fresh, kept)
                left += width

        def scatter(c, fresh, kept):
            nc.vector.tensor_tensor(windows[c][:].indirect(offsets[:]), fresh[:], kept[:], ADD)
            nc.sync.dma_start(out[c * P : (c + 1) * P, :], windows[c][:])

        whole, halving = slice(0, BANK), [BANK // 2, BANK // 4, BANK // 4]

        c = 0
        fresh = work.tile([P, STREAMS], F32, name="fresh")
        kept = work.tile([P, STREAMS], F32, name="kept")
        ps_vn, ps_r, ps_z, ps_un = new_bank(), new_bank(), new_bank(), new_bank()
        w_r, w_z, w_n = (gate_columns(g, c) for g in (R, Z, N))
        first_unit = [(ps_vn, w_n, 0, 2), (ps_r, w_r, 0, 8), (ps_z, w_z, 0, 8), (ps_un, w_n, 2, 8)]
        ps_vn_1, ps_r_1, ps_un_1 = new_bank(), new_bank(), new_bank()
        second_unit = [(ps_vn_1, w_n, 0, 2), (ps_r_1, w_r, 0, 8), (ps_un_1, w_n, 2, 8)]
        for s in range(CTX_SLABS.start):
            multiply(first_unit, 0, only=[s])
            multiply(second_unit, 1, only=[s])

        nc.tensor.transpose(ps_start[:, 0:P], bias_rows[:], identity[:])
        bias_columns = held.tile([P, 6 * BLOCKS], F32, name="bias_columns")
        nc.vector.tensor_copy(bias_columns[:], ps_start[:, 0 : 6 * BLOCKS])
        bias_ih = bias_columns[:, 0 : 3 * BLOCKS]
        bias_hh = bias_columns[:, 3 * BLOCKS : 6 * BLOCKS]
        bias_sum = held.tile([P, 3 * BLOCKS], F32, name="bias_sum")
        nc.vector.tensor_tensor(bias_sum[:], bias_ih, bias_hh, ADD)
        bias_ih_neg = held.tile([P, 3 * BLOCKS], F32, name="bias_ih_neg")
        nc.vector.tensor_scalar_mul(bias_ih_neg[:], bias_ih, -1.0)

        for s in CTX_SLABS:
            multiply(first_unit, 0, only=[s])
        r, z = sigmoid(ps_r, R, c), sigmoid(ps_z, Z, c)
        minus_n = candidate(c, reset(c, ps_vn, r), ps_un)
        mix(c, 0, whole, z, minus_n, fresh, kept)
        multiply(second_unit, 1, only=CTX_SLABS)
        r = sigmoid(ps_r_1, R, c)
        minus_n = candidate(c, reset(c, ps_vn_1, r), ps_un_1)
        z_last(c, 1, halving, minus_n, fresh, kept)
        scatter(c, fresh, kept)

        c = 1
        fresh = work.tile([P, STREAMS], F32, name="fresh")
        kept = work.tile([P, STREAMS], F32, name="kept")
        r_0 = sigmoid(product(R, c, 0, 0, 8), R, c)
        z_0 = sigmoid(product(Z, c, 0, 0, 8), Z, c)
        r_1 = sigmoid(product(R, c, 1, 0, 8), R, c)
        r_vn_0 = reset(c, product(N, c, 0, 0, 2), r_0)
        r_vn_1 = reset(c, product(N, c, 1, 0, 2), r_1)
        minus_n_0 = candidate(c, r_vn_0, product(N, c, 0, 2, 8))
        minus_n = candidate(c, r_vn_1, product(N, c, 1, 2, 8))
        mix(c, 0, whole, z_0, minus_n_0, fresh, kept)
        z_last(c, 1, halving, minus_n, fresh, kept)
        scatter(c, fresh, kept)
